import numpy as np
import ml_dtypes


def mxq(x, axis, fmt="e4m3"):
    dtype, down = {"e4m3": (ml_dtypes.float8_e4m3fn, 7), "e5m2": (ml_dtypes.float8_e5m2, 14)}[fmt]
    v = np.moveaxis(np.asarray(x, np.float32).astype(ml_dtypes.bfloat16).astype(np.float64), axis, -1)
    blocks = v.reshape(v.shape[:-1] + (-1, 32))
    amax = np.abs(blocks).max(-1, keepdims=True)
    byte = np.maximum(np.where(amax > 0, np.frexp(amax)[1] - 1 + 127, 0) - down, 1)
    scale = np.exp2(byte - 127.0)
    codes = (blocks / scale).astype(np.float32).astype(dtype).astype(np.float64)
    return np.moveaxis((codes * scale).reshape(v.shape), -1, axis)


WIDE = False


def mx_kscale(k):
    if not WIDE:
        return np.ones(k)
    levels = np.array([18, -18])
    if k % 512:
        return np.exp2(np.random.permutation(np.resize(levels, k // 32))).repeat(32)
    a = np.empty((k // 512, 16))
    for p in range(k // 512):
        a[p, :8] = np.random.permutation(np.resize(levels, 8))
        for g in range(8):
            far = levels[np.abs(levels - a[p, g]) >= 10]
            a[p, g + 8] = far[np.random.randint(len(far))]
    return np.exp2(a.ravel()).repeat(32)


BF16 = ml_dtypes.bfloat16


def bf(x):
    return np.asarray(x, np.float32).astype(BF16)


def f64(x):
    return np.asarray(x).astype(np.float64)


N, A, D = 2048, 1024, 1024
TEMP = 0.05
EPS = 1e-8


def row_norm(x):
    return np.maximum(np.sqrt((x * x).sum(-1, keepdims=True)), EPS)


def project(d, unit, norm):
    return (d - unit * (d * unit).sum(-1, keepdims=True)) / norm


def setup_inputs():
    s = mx_kscale(N)[:, None]
    u = mx_kscale(A)
    shared = np.random.standard_normal(D)
    emb0 = bf(np.random.standard_normal((N, D)) + np.random.standard_normal((N, 1)) * shared)
    weight0 = bf(np.random.standard_normal((A, D)) + np.random.standard_normal((A, 1)) * shared)
    g = bf(8.0 * np.random.standard_normal((N, A)) * np.exp2(np.random.randint(-6, 1, (N, 1))) / s * u)
    emb_norm = row_norm(f64(emb0))
    weight_norm = row_norm(f64(weight0))
    return {"emb": bf(f64(emb0) * s), "weight": bf(f64(weight0) / u[:, None]),
            "emb_norm": np.asarray(emb_norm, np.float32), "weight_norm": np.asarray(weight_norm, np.float32),
            "grad_out": g}


def reference(emb, weight, emb_norm, weight_norm, grad_out):
    ne = f64(emb_norm)
    nw = f64(weight_norm)
    g = f64(grad_out)
    en = f64(emb) / ne
    wn = f64(weight) / nw
    c = 1.0 / (2.0 * TEMP)
    den = c * (mxq(g, 1, "e5m2") @ mxq(wn, 0, "e4m3"))
    dwn = c * (mxq(g, 0, "e5m2").T @ mxq(en, 0, "e4m3"))
    return project(den, en, ne), project(dwn, wn, nw)

@@ -1,0 +1,361 @@
+from contextlib import ExitStack
+
+import concourse.mybir as mybir
+from concourse.masks import make_identity
+
+N, A, D = 2048, 1024, 1024
+FLOPS = 2 * 2 * N * A * D
+
+F32 = mybir.dt.float32
+BF16 = mybir.dt.bfloat16
+U32 = mybir.dt.uint32
+U8 = mybir.dt.uint8
+E4M3 = mybir.dt.float8_e4m3fn_x4
+E5M2 = mybir.dt.float8_e5m2_x4
+ALU = mybir.AluOpType
+ACT = mybir.ActivationFunctionType
+
+P = 128
+PACK = 4
+KP = P * PACK
+HALF = 512
+TOKEN_PASSES = N // KP
+CLASS_PASSES = A // KP
+FACTOR = 10.0
+SCALAR_TERM_COLS = 832
+STEPS_PER_PASS = 3
+
+
+def tile_classifier_v_kernel(tc, emb, weight, emb_norm, weight_norm, grad_out, out_0, out_1):
+    nc = tc.nc
+    halves = [slice(0, HALF), slice(HALF, D)]
+
+    with ExitStack() as ctx:
+        keep = ctx.enter_context(tc.tile_pool(name="keep", bufs=1))
+        stage = ctx.enter_context(tc.tile_pool(name="stage", bufs=2))
+        psum = ctx.enter_context(tc.psum_pool(name="psum", bufs=8))
+        ctx.enter_context(tc.manual_schedule())
+
+        emb_v = emb.rearrange("(g p j) d -> g p j d", p=P, j=PACK)
+        grad_v = grad_out.rearrange("(g p j) a -> g p j a", p=P, j=PACK)
+        w_v = weight.rearrange("(q p j) d -> q p j d", p=P, j=PACK)
+        w_rows_v = weight.rearrange("(s t p) d -> s p t d", p=P, t=2)
+        out0_v = out_0.rearrange("(g p j) d -> g j p d", p=P, j=PACK)
+        out1_v = out_1.rearrange("(t p) d -> t p d", p=P)
+
+        w_norm = keep.tile([P, CLASS_PASSES, PACK], F32)
+        nc.sync.dma_start(out=w_norm[:], in_=weight_norm.rearrange("(q p j) o -> p q (j o)", p=P, j=PACK))
+        w_raw = {}
+        g_raw = {}
+        e_raw = {}
+
+        def load_w(q, h):
+            w_raw[q, h] = stage.tile([P, PACK, HALF], BF16, name="w_raw", bufs=4, align_bytes=64)
+            nc.sync.dma_start(out=w_raw[q, h][:], in_=w_v[q][:, :, halves[h]])
+
+        def load_g(g):
+            g_raw[g] = stage.tile([P, PACK, A], BF16, name="g_raw", bufs=4, align_bytes=64)
+            nc.sync.dma_start(out=g_raw[g][:], in_=grad_v[g])
+
+        def load_e(g):
+            e_raw[g] = stage.tile([P, PACK, D], BF16, name="e_raw", bufs=4, align_bytes=64)
+            nc.sync.dma_start(out=e_raw[g][:], in_=emb_v[g])
+
+        load_w(0, 0)
+        load_g(0)
+        load_w(1, 0)
+        load_w(0, 1)
+        load_w(1, 1)
+        e_norm = keep.tile([P, TOKEN_PASSES, PACK], F32)
+        nc.sync.dma_start(out=e_norm[:], in_=emb_norm.rearrange("(g p j) o -> p g (j o)", p=P, j=PACK))
+        load_e(0)
+        for g in range(1, TOKEN_PASSES):
+            load_g(g)
+            load_e(g)
+        row_norm = keep.tile([P, A // P], F32)
+        with nc.allow_non_contiguous_dma(reason="one norm for each partition and class tile"):
+            nc.sync.dma_start(out=row_norm[:], in_=weight_norm.rearrange("(t p) o -> p (t o)", p=P))
+
+        ident = keep.tile([P, P], F32)
+        make_identity(nc, ident[:])
+
+        w_codes = keep.tile([P, CLASS_PASSES, D], U32, align_bytes=64)
+        w_scales = keep.tile([P, CLASS_PASSES, D], U8, align_bytes=64)
+        gt_codes = keep.tile([P, N // P // 2, 2 * CLASS_PASSES * P], U32, align_bytes=64)
+        gt_scales = keep.tile([P, N // P // 2, 2 * CLASS_PASSES * P], U8, align_bytes=64)
+        g_codes = keep.tile([P, TOKEN_PASSES, A], U32, align_bytes=64)
+        g_scales = keep.tile([P, TOKEN_PASSES, A], U8, align_bytes=64)
+        e_codes = keep.tile([P, TOKEN_PASSES, D], U32, align_bytes=64)
+        e_scales = keep.tile([P, TOKEN_PASSES, D], U8, align_bytes=64)
+
+        def row_constants(norm, width, name):
+            inv = keep.tile([P, width], F32, name=name + "_inv")
+            gain = keep.tile([P, width], F32, name=name + "_gain")
+            pull = keep.tile([P, width], F32, name=name + "_pull")
+            nc.vector.reciprocal(out=inv[:], in_=norm)
+            nc.vector.tensor_scalar(out=gain[:], in0=inv[:], scalar1=FACTOR, scalar2=None, op0=ALU.mult)
+            nc.vector.scalar_tensor_tensor(
+                out=pull[:], in0=inv[:], scalar=-FACTOR, in1=inv[:], op0=ALU.mult, op1=ALU.mult
+            )
+            return inv, gain, pull
+
+        unit = {}
+        grouped = {}
+        flipped = {}
+
+        def normalise(key, raw, inv, first, slots):
+            if key not in unit:
+                unit[key] = stage.tile(list(raw.shape), BF16, name="unit", bufs=2, align_bytes=64)
+            for j in slots:
+                nc.vector.tensor_scalar(
+                    out=unit[key][:, j, :], in0=raw[:, j, :], scalar1=inv[:, first + j : first + j + 1],
+                    scalar2=None, op0=ALU.mult,
+                )
+
+        def interleave(key, src, on_vector):
+            grouped[key] = stage.tile([P, HALF, PACK], BF16, name="grouped", bufs=4, align_bytes=64)
+            dst_v = grouped[key][:].rearrange("p (c i) j -> p c j i", i=4)
+            src_v = src.rearrange("p j (c i) -> p c j i", i=4)
+            if on_vector:
+                nc.vector.tensor_copy(out=dst_v, in_=src_v)
+            else:
+                nc.scalar.copy(out=dst_v, in_=src_v)
+
+        def quantise(key, codes, scales, fmt):
+            nc.vector.quantize_mx(
+                out=codes.bitcast(fmt), scales=scales, in_=grouped[key][:].rearrange("p c j -> p (c j)")
+            )
+
+        tr_bank = {}
+
+        def transpose_pair(pair):
+            for i in (2 * pair, 2 * pair + 1):
+                g, j = divmod(i, PACK)
+                words = g_raw[g][:, j, :].bitcast(F32)
+                tr_bank[i] = psum.tile([P, HALF], F32, name="bank")
+                for q in range(CLASS_PASSES):
+                    for u in range(2):
+                        col = (2 * q + u) * P
+                        nc.tensor.transpose(
+                            tr_bank[i][:, col : col + P], words[:, 256 * q + u : 256 * (q + 1) : 2], ident[:]
+                        )
+
+        def copy_pair(pair):
+            flipped[pair] = stage.tile([P, 2, A], BF16, name="flipped", bufs=2, align_bytes=64)
+            for s in range(2):
+                nc.scalar.copy(
+                    out=flipped[pair][:, s, :].bitcast(F32).rearrange("p (q r u) -> p q r u", q=CLASS_PASSES, u=2),
+                    in_=tr_bank[2 * pair + s][:].rearrange("p (q u r) -> p q r u", q=CLASS_PASSES, u=2),
+                )
+
+        def quantise_pair(pair):
+            nc.vector.quantize_mx(
+                out=gt_codes[:, pair, :].bitcast(E5M2), scales=gt_scales[:, pair, :],
+                in_=flipped[pair][:].rearrange("p s a -> p (s a)"),
+            )
+
+        w_rows = {}
+
+        def load_w_rows(s):
+            w_rows[s] = stage.tile([P, 2, D], BF16, name="w_raw", bufs=4, align_bytes=64)
+            nc.sync.dma_start(out=w_rows[s][:], in_=w_rows_v[s])
+
+        acc = {}
+        res = {}
+        sums = {}
+        coef = {}
+        term = {}
+        consts = {}
+
+        def rows_of(tile):
+            kind, i = tile
+            if kind == "emb":
+                return e_raw[i // PACK][:, i % PACK, :]
+            return w_rows[i // 2][:, i % 2, :]
+
+        def const_of(tile, which):
+            kind, i = tile
+            return consts[kind][which][:, i : i + 1]
+
+        def multiply(tile):
+            kind, i = tile
+            for h in range(2):
+                acc[tile, h] = psum.tile([P, HALF], F32, name="bank")
+                passes = CLASS_PASSES if kind == "emb" else TOKEN_PASSES
+                for k in range(passes):
+                    if kind == "emb":
+                        c0 = ((i % 2) * CLASS_PASSES + k) * P
+                        lhs, lhs_s = gt_codes[:, i // 2, c0 : c0 + P], gt_scales[:, i // 2, c0 : c0 + P]
+                        rhs, rhs_s = w_codes[:, k, halves[h]], w_scales[:, k, halves[h]]
+                    else:
+                        lhs, lhs_s = g_codes[:, k, i * P : (i + 1) * P], g_scales[:, k, i * P : (i + 1) * P]
+                        rhs, rhs_s = e_codes[:, k, halves[h]], e_scales[:, k, halves[h]]
+                    nc.tensor.matmul_mx(
+                        out=acc[tile, h][:], lhsT=lhs.bitcast(E5M2), lhsT_scale=lhs_s,
+                        rhs=rhs.bitcast(E4M3), rhs_scale=rhs_s, start=(k == 0), stop=(k == passes - 1),
+                    )
+
+        def row_sums(tile):
+            res[tile] = stage.tile([P, D], F32, name="res", bufs=6)
+            sums[tile] = stage.tile([P, 2], F32, name="sums", bufs=4)
+            for h in range(2):
+                nc.vector.scalar_tensor_tensor(
+                    out=res[tile][:, halves[h]], in0=acc[tile, h][:], scalar=const_of(tile, 0),
+                    in1=rows_of(tile)[:, halves[h]], op0=ALU.mult, op1=ALU.mult,
+                    accum_out=sums[tile][:, h : h + 1],
+                )
+
+        def coefficient(tile, engine):
+            coef[tile] = stage.tile([P, 1], F32, name="coef", bufs=4)
+            term[tile] = stage.tile([P, D], F32, name="term", bufs=3)
+            engine.tensor_scalar(
+                out=coef[tile][:], in0=sums[tile][:, 0:1], scalar1=sums[tile][:, 1:2], scalar2=const_of(tile, 2),
+                op0=ALU.add, op1=ALU.mult,
+            )
+
+        def term_gpsimd(tile, cols):
+            nc.gpsimd.tensor_scalar(
+                out=term[tile][:, cols], in0=rows_of(tile)[:, cols], scalar1=coef[tile][:], scalar2=1.0,
+                op0=ALU.mult, op1=ALU.mult,
+            )
+
+        def term_scalar(tile, cols):
+            nc.scalar.activation(
+                out=term[tile][:, cols], in_=rows_of(tile)[:, cols], func=ACT.Copy, scale=coef[tile][:]
+            )
+
+        def finish_vector(tile, h):
+            nc.vector.scalar_tensor_tensor(
+                out=res[tile][:, halves[h]], in0=acc[tile, h][:], scalar=const_of(tile, 1),
+                in1=term[tile][:, halves[h]], op0=ALU.mult, op1=ALU.add,
+            )
+
+        def scale_scalar(tile):
+            nc.scalar.activation(
+                out=res[tile][:, halves[1]], in_=acc[tile, 1][:], func=ACT.Copy, scale=const_of(tile, 1)
+            )
+
+        def finish_gpsimd(tile):
+            nc.gpsimd.tensor_tensor(
+                out=res[tile][:, halves[1]], in0=res[tile][:, halves[1]], in1=term[tile][:, halves[1]], op=ALU.add
+            )
+
+        def store(tile):
+            kind, i = tile
+            dst = out0_v[i // PACK][i % PACK] if kind == "emb" else out1_v[i]
+            nc.sync.dma_start(out=dst, in_=res[tile][:])
+
+        w_inv = keep.tile([P, CLASS_PASSES * PACK], F32)
+        nc.vector.reciprocal(out=w_inv[:], in_=w_norm[:].rearrange("p q j -> p (q j)"))
+
+        def w_normalise(q, h):
+            normalise(("w", q, h), w_raw[q, h], w_inv, q * PACK, range(PACK))
+
+        def w_interleave(q, h, on_vector):
+            interleave(("w", q, h), unit["w", q, h][:], on_vector)
+
+        def w_quantise(q, h):
+            quantise(("w", q, h), w_codes[:, q, halves[h]], w_scales[:, q, halves[h]], E4M3)
+
+        w_normalise(0, 0)
+        w_interleave(0, 0, False)
+        transpose_pair(0)
+        transpose_pair(1)
+        copy_pair(0)
+        copy_pair(1)
+        w_normalise(1, 0)
+        w_quantise(0, 0)
+        w_interleave(1, 0, True)
+        w_normalise(0, 1)
+        w_quantise(1, 0)
+        w_interleave(0, 1, True)
+        w_normalise(1, 1)
+        w_quantise(0, 1)
+        w_interleave(1, 1, True)
+        quantise_pair(0)
+        w_quantise(1, 1)
+        consts["emb"] = row_constants(e_norm[:].rearrange("p g j -> p (g j)"), N // P, "emb")
+
+        early = TOKEN_PASSES * STEPS_PER_PASS
+        order = [("emb", i) for i in range(early + 2)]
+        late_emb = list(range(early + 2, N // P))
+        for m in range(A // P):
+            order.append(("w", m))
+            if m < len(late_emb):
+                order.append(("emb", late_emb[m]))
+
+        def g_interleave(g, h):
+            interleave(("g", g, h), g_raw[g][:, :, halves[h]], False)
+
+        def e_interleave(g, h):
+            interleave(("e", g, h), unit["e", g][:, :, halves[h]], False)
+
+        def g_quantise(g, h):
+            quantise(("g", g, h), g_codes[:, g, halves[h]], g_scales[:, g, halves[h]], E5M2)
+
+        def e_quantise(g, h):
+            quantise(("e", g, h), e_codes[:, g, halves[h]], e_scales[:, g, halves[h]], E4M3)
+
+        multiply(order[0])
+        for step in range(early + 1):
+            g, part = divmod(step, STEPS_PER_PASS)
+            last = g + 1 >= TOKEN_PASSES
+            if part == 0:
+                if g > 0:
+                    e_quantise(g - 1, 0)
+                if g < TOKEN_PASSES:
+                    quantise_pair(2 * g + 1)
+                    normalise(("e", g), e_raw[g], consts["emb"][0], g * PACK, range(PACK))
+                    g_interleave(g, 0)
+                else:
+                    e_quantise(g - 1, 1)
+            elif part == 1:
+                if g > 0:
+                    e_quantise(g - 1, 1)
+                g_quantise(g, 0)
+                g_interleave(g, 1)
+            else:
+                g_quantise(g, 1)
+                if not last:
+                    quantise_pair(2 * g + 2)
+            multiply(order[step + 1])
+            if part == 0 and not last:
+                transpose_pair(2 * g + 2)
+            if part == 1:
+                if not last:
+                    copy_pair(2 * g + 2)
+                    transpose_pair(2 * g + 3)
+                e_interleave(g, 0)
+            if part == 2:
+                if not last:
+                    copy_pair(2 * g + 3)
+                e_interleave(g, 1)
+            if step > 0:
+                coefficient(order[step - 1], nc.vector)
+                for h in range(2):
+                    term_gpsimd(order[step - 1], halves[h])
+            row_sums(order[step])
+            if step > 0:
+                for h in range(2):
+                    finish_vector(order[step - 1], h)
+                store(order[step - 1])
+            if 4 <= step < 8:
+                load_w_rows(step - 4)
+            if step == 8:
+                consts["w"] = row_constants(row_norm[:], A // P, "w")
+
+        for step in range(early, len(order) + 1):
+            if step < len(order):
+                tile = order[step]
+                if step > early:
+                    if step + 1 < len(order):
+                        multiply(order[step + 1])
+                    row_sums(tile)
+                scale_scalar(tile)
+                coefficient(tile, nc.gpsimd)
+                term_gpsimd(tile, slice(SCALAR_TERM_COLS, D))
+                term_scalar(tile, slice(0, SCALAR_TERM_COLS))
+            if step > early:
+                finish_vector(order[step - 1], 0)
+                finish_gpsimd(order[step - 1])
+                store(order[step - 1])

@@ -22,7 +22,6 @@ HALF = 512
 TOKEN_PASSES = N // KP
 CLASS_PASSES = A // KP
 FACTOR = 10.0
-SCALAR_TERM_COLS = 832
 STEPS_PER_PASS = 3
 
 
@@ -44,7 +43,9 @@ def tile_classifier_v_kernel(tc, emb, weight, emb_norm, weight_norm, grad_out, o
         out1_v = out_1.rearrange("(t p) d -> t p d", p=P)
 
         w_norm = keep.tile([P, CLASS_PASSES, PACK], F32)
-        nc.sync.dma_start(out=w_norm[:], in_=weight_norm.rearrange("(q p j) o -> p q (j o)", p=P, j=PACK))
+        nc.scalar.dma_start(out=w_norm[:], in_=weight_norm.rearrange("(q p j) o -> p q (j o)", p=P, j=PACK))
+        e_norm = keep.tile([P, TOKEN_PASSES, PACK], F32)
+        nc.scalar.dma_start(out=e_norm[:], in_=emb_norm.rearrange("(g p j) o -> p g (j o)", p=P, j=PACK))
         w_raw = {}
         g_raw = {}
         e_raw = {}
@@ -54,7 +55,7 @@ def tile_classifier_v_kernel(tc, emb, weight, emb_norm, weight_norm, grad_out, o
             nc.sync.dma_start(out=w_raw[q, h][:], in_=w_v[q][:, :, halves[h]])
 
         def load_g(g):
-            g_raw[g] = stage.tile([P, PACK, A], BF16, name="g_raw", bufs=4, align_bytes=64)
+            g_raw[g] = stage.tile([P, PACK, A], BF16, name="g_raw", bufs=3, align_bytes=64)
             nc.sync.dma_start(out=g_raw[g][:], in_=grad_v[g])
 
         def load_e(g):
@@ -62,15 +63,14 @@ def tile_classifier_v_kernel(tc, emb, weight, emb_norm, weight_norm, grad_out, o
             nc.sync.dma_start(out=e_raw[g][:], in_=emb_v[g])
 
         load_w(0, 0)
-        load_g(0)
         load_w(1, 0)
         load_w(0, 1)
+        load_g(0)
         load_w(1, 1)
-        e_norm = keep.tile([P, TOKEN_PASSES, PACK], F32)
-        nc.sync.dma_start(out=e_norm[:], in_=emb_norm.rearrange("(g p j) o -> p g (j o)", p=P, j=PACK))
         load_e(0)
         for g in range(1, TOKEN_PASSES):
-            load_g(g)
+            if g + 1 < TOKEN_PASSES:
+                load_g(g)
             load_e(g)
         row_norm = keep.tile([P, A // P], F32)
         with nc.allow_non_contiguous_dma(reason="one norm for each partition and class tile"):
@@ -88,16 +88,24 @@ def tile_classifier_v_kernel(tc, emb, weight, emb_norm, weight_norm, grad_out, o
         e_codes = keep.tile([P, TOKEN_PASSES, D], U32, align_bytes=64)
         e_scales = keep.tile([P, TOKEN_PASSES, D], U8, align_bytes=64)
 
-        def row_constants(norm, width, name):
-            inv = keep.tile([P, width], F32, name=name + "_inv")
+        def inverse(norm, width, name):
+            inv = keep.tile([P, width], F32, name=name)
+            nc.vector.reciprocal(out=inv[:], in_=norm)
+            return inv
+
+        def row_constants(inv, width, name):
             gain = keep.tile([P, width], F32, name=name + "_gain")
             pull = keep.tile([P, width], F32, name=name + "_pull")
-            nc.vector.reciprocal(out=inv[:], in_=norm)
             nc.vector.tensor_scalar(out=gain[:], in0=inv[:], scalar1=FACTOR, scalar2=None, op0=ALU.mult)
             nc.vector.scalar_tensor_tensor(
                 out=pull[:], in0=inv[:], scalar=-FACTOR, in1=inv[:], op0=ALU.mult, op1=ALU.mult
             )
             return inv, gain, pull
+
+        def negated(inv, width):
+            neg = keep.tile([P, width], F32)
+            nc.vector.tensor_scalar(out=neg[:], in0=inv[:], scalar1=-1.0, scalar2=None, op0=ALU.mult)
+            return neg
 
         unit = {}
         grouped = {}
@@ -105,7 +113,7 @@ def tile_classifier_v_kernel(tc, emb, weight, emb_norm, weight_norm, grad_out, o
 
         def normalise(key, raw, inv, first, slots):
             if key not in unit:
-                unit[key] = stage.tile(list(raw.shape), BF16, name="unit", bufs=2, align_bytes=64)
+                unit[key] = stage.tile(list(raw.shape), BF16, name="unit", bufs=3, align_bytes=64)
             for j in slots:
                 nc.vector.tensor_scalar(
                     out=unit[key][:, j, :], in0=raw[:, j, :], scalar1=inv[:, first + j : first + j + 1],
@@ -177,12 +185,17 @@ def tile_classifier_v_kernel(tc, emb, weight, emb_norm, weight_norm, grad_out, o
             kind, i = tile
             return consts[kind][which][:, i : i + 1]
 
-        def multiply(tile):
+        begun = {}
+
+        def multiply(tile, upto=None):
             kind, i = tile
+            passes = CLASS_PASSES if kind == "emb" else TOKEN_PASSES
+            first = begun.get(tile, 0)
+            begun[tile] = passes if upto is None else upto
             for h in range(2):
-                acc[tile, h] = psum.tile([P, HALF], F32, name="bank")
-                passes = CLASS_PASSES if kind == "emb" else TOKEN_PASSES
-                for k in range(passes):
+                if first == 0:
+                    acc[tile, h] = psum.tile([P, HALF], F32, name="bank")
+                for k in range(first, begun[tile]):
                     if kind == "emb":
                         c0 = ((i % 2) * CLASS_PASSES + k) * P
                         lhs, lhs_s = gt_codes[:, i // 2, c0 : c0 + P], gt_scales[:, i // 2, c0 : c0 + P]
@@ -205,18 +218,30 @@ def tile_classifier_v_kernel(tc, emb, weight, emb_norm, weight_norm, grad_out, o
                     accum_out=sums[tile][:, h : h + 1],
                 )
 
-        def coefficient(tile, engine):
+        def early_coefficient(tile):
             coef[tile] = stage.tile([P, 1], F32, name="coef", bufs=4)
-            term[tile] = stage.tile([P, D], F32, name="term", bufs=3)
-            engine.tensor_scalar(
-                out=coef[tile][:], in0=sums[tile][:, 0:1], scalar1=sums[tile][:, 1:2], scalar2=const_of(tile, 2),
-                op0=ALU.add, op1=ALU.mult,
+            nc.vector.tensor_scalar(
+                out=coef[tile][:], in0=sums[tile][:, 0:1], scalar1=sums[tile][:, 1:2],
+                scalar2=e_neg_inv[:, tile[1] : tile[1] + 1], op0=ALU.add, op1=ALU.mult,
             )
 
-        def term_gpsimd(tile, cols):
-            nc.gpsimd.tensor_scalar(
-                out=term[tile][:, cols], in0=rows_of(tile)[:, cols], scalar1=coef[tile][:], scalar2=1.0,
-                op0=ALU.mult, op1=ALU.mult,
+        def early_finish(tile):
+            for h in range(2):
+                nc.vector.scalar_tensor_tensor(
+                    out=res[tile][:, halves[h]], in0=rows_of(tile)[:, halves[h]], scalar=coef[tile][:],
+                    in1=acc[tile, h][:], op0=ALU.mult, op1=ALU.add,
+                )
+                nc.gpsimd.tensor_scalar(
+                    out=res[tile][:, halves[h]], in0=res[tile][:, halves[h]], scalar1=const_of(tile, 1),
+                    scalar2=1.0, op0=ALU.mult, op1=ALU.mult,
+                )
+
+        def late_coefficient(tile):
+            coef[tile] = stage.tile([P, 1], F32, name="coef", bufs=4)
+            parts = stage.tile([P, 2], F32, name="parts", bufs=2)
+            term[tile] = stage.tile([P, D], F32, name="term", bufs=3)
+            nc.scalar.activation(
+                out=parts[:], in_=sums[tile][:], func=ACT.Copy, scale=const_of(tile, 2), accum_out=coef[tile][:]
             )
 
         def term_scalar(tile, cols):
@@ -240,13 +265,12 @@ def tile_classifier_v_kernel(tc, emb, weight, emb_norm, weight_norm, grad_out, o
                 out=res[tile][:, halves[1]], in0=res[tile][:, halves[1]], in1=term[tile][:, halves[1]], op=ALU.add
             )
 
-        def store(tile):
+        def store(tile, cols=slice(0, D)):
             kind, i = tile
             dst = out0_v[i // PACK][i % PACK] if kind == "emb" else out1_v[i]
-            nc.sync.dma_start(out=dst, in_=res[tile][:])
+            nc.sync.dma_start(out=dst[:, cols], in_=res[tile][:, cols])
 
-        w_inv = keep.tile([P, CLASS_PASSES * PACK], F32)
-        nc.vector.reciprocal(out=w_inv[:], in_=w_norm[:].rearrange("p q j -> p (q j)"))
+        w_inv = inverse(w_norm[:].rearrange("p q j -> p (q j)"), CLASS_PASSES * PACK, "w_inv")
 
         def w_normalise(q, h):
             normalise(("w", q, h), w_raw[q, h], w_inv, q * PACK, range(PACK))
@@ -259,30 +283,29 @@ def tile_classifier_v_kernel(tc, emb, weight, emb_norm, weight_norm, grad_out, o
 
         w_normalise(0, 0)
         w_interleave(0, 0, False)
+        e_inv = inverse(e_norm[:].rearrange("p g j -> p (g j)"), N // P, "e_inv")
+        w_normalise(1, 0)
+        consts["emb"] = row_constants(e_inv, N // P, "emb")
+        e_neg_inv = negated(e_inv, N // P)
+        w_normalise(0, 1)
+        w_interleave(0, 1, False)
+        w_interleave(1, 0, True)
         transpose_pair(0)
         transpose_pair(1)
         copy_pair(0)
-        copy_pair(1)
-        w_normalise(1, 0)
         w_quantise(0, 0)
-        w_interleave(1, 0, True)
-        w_normalise(0, 1)
         w_quantise(1, 0)
-        w_interleave(0, 1, True)
         w_normalise(1, 1)
         w_quantise(0, 1)
         w_interleave(1, 1, True)
         quantise_pair(0)
         w_quantise(1, 1)
-        consts["emb"] = row_constants(e_norm[:].rearrange("p g j -> p (g j)"), N // P, "emb")
 
         early = TOKEN_PASSES * STEPS_PER_PASS
-        order = [("emb", i) for i in range(early + 2)]
-        late_emb = list(range(early + 2, N // P))
-        for m in range(A // P):
-            order.append(("w", m))
-            if m < len(late_emb):
-                order.append(("emb", late_emb[m]))
+        order = [("emb", i) for i in range(early)]
+        for i in range(early, N // P):
+            m = 2 * (i - early)
+            order.extend([("emb", i), ("w", m), ("w", m + 1)])
 
         def g_interleave(g, h):
             interleave(("g", g, h), g_raw[g][:, :, halves[h]], False)
@@ -296,28 +319,59 @@ def tile_classifier_v_kernel(tc, emb, weight, emb_norm, weight_norm, grad_out, o
         def e_quantise(g, h):
             quantise(("e", g, h), e_codes[:, g, halves[h]], e_scales[:, g, halves[h]], E4M3)
 
+        def e_normalise(g, slots):
+            normalise(("e", g), e_raw[g], consts["emb"][0], g * PACK, slots)
+
+        def vector_chunk(step):
+            g, part = divmod(step, STEPS_PER_PASS)
+            calls = []
+            if part == 0:
+                if g > 0:
+                    calls.append(lambda: e_quantise(g - 1, 0))
+                if g < TOKEN_PASSES:
+                    calls.append(lambda: e_normalise(g, range(PACK)))
+                    if g > 0:
+                        calls.append(lambda: quantise_pair(2 * g + 1))
+                else:
+                    calls.append(lambda: e_quantise(g - 1, 1))
+            elif part == 1:
+                if g > 0:
+                    calls.append(lambda: e_quantise(g - 1, 1))
+                else:
+                    calls.append(lambda: quantise_pair(1))
+                calls.append(lambda: g_quantise(g, 0))
+            else:
+                calls.append(lambda: g_quantise(g, 1))
+                if g + 1 < TOKEN_PASSES:
+                    calls.append(lambda: quantise_pair(2 * g + 2))
+            return calls
+
+        def late_start(tile):
+            late_coefficient(tile)
+            scale_scalar(tile)
+            term_scalar(tile, slice(0, D))
+            finish_gpsimd(tile)
+
+        busy = early - 1
         multiply(order[0])
         for step in range(early + 1):
             g, part = divmod(step, STEPS_PER_PASS)
             last = g + 1 >= TOKEN_PASSES
-            if part == 0:
-                if g > 0:
-                    e_quantise(g - 1, 0)
-                if g < TOKEN_PASSES:
-                    quantise_pair(2 * g + 1)
-                    normalise(("e", g), e_raw[g], consts["emb"][0], g * PACK, range(PACK))
-                    g_interleave(g, 0)
-                else:
-                    e_quantise(g - 1, 1)
-            elif part == 1:
-                if g > 0:
-                    e_quantise(g - 1, 1)
-                g_quantise(g, 0)
+            chunk = vector_chunk(step)
+            finish_early = 0 < step <= busy
+            if finish_early and len(chunk) == 1:
+                early_coefficient(order[step - 1])
+            chunk[0]()
+            if finish_early and len(chunk) > 1:
+                early_coefficient(order[step - 1])
+            for call in chunk[1:]:
+                call()
+            if part == 0 and g < TOKEN_PASSES:
+                g_interleave(g, 0)
+            if step == 0:
+                copy_pair(1)
+            if part == 1:
                 g_interleave(g, 1)
-            else:
-                g_quantise(g, 1)
-                if not last:
-                    quantise_pair(2 * g + 2)
             multiply(order[step + 1])
             if part == 0 and not last:
                 transpose_pair(2 * g + 2)
@@ -329,33 +383,43 @@ def tile_classifier_v_kernel(tc, emb, weight, emb_norm, weight_norm, grad_out, o
             if part == 2:
                 if not last:
                     copy_pair(2 * g + 3)
+                else:
+                    multiply(("w", 0), upto=TOKEN_PASSES - 1)
                 e_interleave(g, 1)
-            if step > 0:
-                coefficient(order[step - 1], nc.vector)
-                for h in range(2):
-                    term_gpsimd(order[step - 1], halves[h])
-            row_sums(order[step])
-            if step > 0:
-                for h in range(2):
-                    finish_vector(order[step - 1], h)
+            if finish_early:
+                early_finish(order[step - 1])
                 store(order[step - 1])
+            row_sums(order[step])
+            if step >= busy:
+                late_start(order[step])
+            if step == 1:
+                load_g(TOKEN_PASSES - 1)
             if 4 <= step < 8:
                 load_w_rows(step - 4)
+            if step == 7:
+                row_inv = inverse(row_norm[:], A // P, "row_inv")
             if step == 8:
-                consts["w"] = row_constants(row_norm[:], A // P, "w")
+                consts["w"] = row_constants(row_inv, A // P, "w")
 
-        for step in range(early, len(order) + 1):
-            if step < len(order):
-                tile = order[step]
-                if step > early:
-                    if step + 1 < len(order):
-                        multiply(order[step + 1])
-                    row_sums(tile)
-                scale_scalar(tile)
-                coefficient(tile, nc.gpsimd)
-                term_gpsimd(tile, slice(SCALAR_TERM_COLS, D))
-                term_scalar(tile, slice(0, SCALAR_TERM_COLS))
-            if step > early:
-                finish_vector(order[step - 1], 0)
-                finish_gpsimd(order[step - 1])
-                store(order[step - 1])
+        final = len(order) - 1
+        store(order[busy], halves[1])
+        for step in range(early + 1, final):
+            multiply(order[step + 1])
+            row_sums(order[step])
+            late_start(order[step])
+            finish_vector(order[step - 2], 0)
+            store(order[step - 2], halves[0])
+            store(order[step - 1], halves[1])
+        tile = order[final]
+        row_sums(tile)
+        late_coefficient(tile)
+        term_scalar(tile, halves[0])
+        term_scalar(tile, halves[1])
+        finish_vector(order[final - 2], 0)
+        store(order[final - 2], halves[0])
+        finish_vector(order[final - 1], 0)
+        for h in range(2):
+            store(order[final - 1], halves[h])
+        for h in range(2):
+            finish_vector(tile, h)
+            store(tile, halves[h])

@@ -22,7 +22,8 @@ HALF = 512
 TOKEN_PASSES = N // KP
 CLASS_PASSES = A // KP
 FACTOR = 10.0
-STEPS_PER_PASS = 3
+WINDOW_TILES = (3, 2, 2, 2)
+GPSIMD_COLS = (1024, 64, 320, 320)
 
 
 def tile_classifier_v_kernel(tc, emb, weight, emb_norm, weight_norm, grad_out, out_0, out_1):
@@ -81,8 +82,8 @@ def tile_classifier_v_kernel(tc, emb, weight, emb_norm, weight_norm, grad_out, o
 
         w_codes = keep.tile([P, CLASS_PASSES, D], U32, align_bytes=64)
         w_scales = keep.tile([P, CLASS_PASSES, D], U8, align_bytes=64)
-        gt_codes = keep.tile([P, N // P // 2, 2 * CLASS_PASSES * P], U32, align_bytes=64)
-        gt_scales = keep.tile([P, N // P // 2, 2 * CLASS_PASSES * P], U8, align_bytes=64)
+        gt_codes = keep.tile([P, TOKEN_PASSES, PACK, CLASS_PASSES * P], U32, align_bytes=64)
+        gt_scales = keep.tile([P, TOKEN_PASSES, PACK, CLASS_PASSES * P], U8, align_bytes=64)
         g_codes = keep.tile([P, TOKEN_PASSES, A], U32, align_bytes=64)
         g_scales = keep.tile([P, TOKEN_PASSES, A], U8, align_bytes=64)
         e_codes = keep.tile([P, TOKEN_PASSES, D], U32, align_bytes=64)
@@ -111,27 +112,33 @@ def tile_classifier_v_kernel(tc, emb, weight, emb_norm, weight_norm, grad_out, o
         grouped = {}
         flipped = {}
 
-        def normalise(key, raw, inv, first, slots):
-            if key not in unit:
-                unit[key] = stage.tile(list(raw.shape), BF16, name="unit", bufs=3, align_bytes=64)
-            for j in slots:
+        def normalise(dst, raw, inv, first):
+            for j in range(PACK):
                 nc.vector.tensor_scalar(
-                    out=unit[key][:, j, :], in0=raw[:, j, :], scalar1=inv[:, first + j : first + j + 1],
+                    out=dst[:, j, :], in0=raw[:, j, :], scalar1=inv[:, first + j : first + j + 1],
                     scalar2=None, op0=ALU.mult,
                 )
 
-        def interleave(key, src, on_vector):
-            grouped[key] = stage.tile([P, HALF, PACK], BF16, name="grouped", bufs=4, align_bytes=64)
-            dst_v = grouped[key][:].rearrange("p (c i) j -> p c j i", i=4)
+        def interleave(key, src, cols, engine):
+            if key not in grouped:
+                grouped[key] = stage.tile([P, D, PACK], BF16, name="grouped", bufs=4, align_bytes=64)
+            if engine == "gpsimd":
+                nc.gpsimd.tensor_scalar(
+                    out=grouped[key][:, cols, :], in0=src.rearrange("p j c -> p c j"),
+                    scalar1=1.0, scalar2=0.0, op0=ALU.mult, op1=ALU.add,
+                )
+                return
+            dst_v = grouped[key][:, cols, :].rearrange("p (c i) j -> p c j i", i=4)
             src_v = src.rearrange("p j (c i) -> p c j i", i=4)
-            if on_vector:
+            if engine == "vector":
                 nc.vector.tensor_copy(out=dst_v, in_=src_v)
             else:
                 nc.scalar.copy(out=dst_v, in_=src_v)
 
-        def quantise(key, codes, scales, fmt):
+        def quantise(key, cols, codes, scales, fmt):
             nc.vector.quantize_mx(
-                out=codes.bitcast(fmt), scales=scales, in_=grouped[key][:].rearrange("p c j -> p (c j)")
+                out=codes[:, cols].bitcast(fmt), scales=scales[:, cols],
+                in_=grouped[key][:, cols, :].rearrange("p c j -> p (c j)"),
             )
 
         tr_bank = {}
@@ -149,17 +156,20 @@ def tile_classifier_v_kernel(tc, emb, weight, emb_norm, weight_norm, grad_out, o
                         )
 
         def copy_pair(pair):
-            flipped[pair] = stage.tile([P, 2, A], BF16, name="flipped", bufs=2, align_bytes=64)
-            for s in range(2):
+            g = pair // 2
+            if g not in flipped:
+                flipped[g] = stage.tile([P, PACK, A], BF16, name="flipped", bufs=1, align_bytes=64)
+            for i in (2 * pair, 2 * pair + 1):
                 nc.scalar.copy(
-                    out=flipped[pair][:, s, :].bitcast(F32).rearrange("p (q r u) -> p q r u", q=CLASS_PASSES, u=2),
-                    in_=tr_bank[2 * pair + s][:].rearrange("p (q u r) -> p q r u", q=CLASS_PASSES, u=2),
+                    out=flipped[g][:, i % PACK, :].bitcast(F32).rearrange("p (q r u) -> p q r u", q=CLASS_PASSES, u=2),
+                    in_=tr_bank[i][:].rearrange("p (q u r) -> p q r u", q=CLASS_PASSES, u=2),
                 )
 
-        def quantise_pair(pair):
+        def quantise_flipped(g, slots):
             nc.vector.quantize_mx(
-                out=gt_codes[:, pair, :].bitcast(E5M2), scales=gt_scales[:, pair, :],
-                in_=flipped[pair][:].rearrange("p s a -> p (s a)"),
+                out=gt_codes[:, g, slots, :].rearrange("p j c -> p (j c)").bitcast(E5M2),
+                scales=gt_scales[:, g, slots, :].rearrange("p j c -> p (j c)"),
+                in_=flipped[g][:, slots, :].rearrange("p j a -> p (j a)"),
             )
 
         w_rows = {}
@@ -197,8 +207,8 @@ def tile_classifier_v_kernel(tc, emb, weight, emb_norm, weight_norm, grad_out, o
                     acc[tile, h] = psum.tile([P, HALF], F32, name="bank")
                 for k in range(first, begun[tile]):
                     if kind == "emb":
-                        c0 = ((i % 2) * CLASS_PASSES + k) * P
-                        lhs, lhs_s = gt_codes[:, i // 2, c0 : c0 + P], gt_scales[:, i // 2, c0 : c0 + P]
+                        g, j = divmod(i, PACK)
+                        lhs, lhs_s = gt_codes[:, g, j, k * P : (k + 1) * P], gt_scales[:, g, j, k * P : (k + 1) * P]
                         rhs, rhs_s = w_codes[:, k, halves[h]], w_scales[:, k, halves[h]]
                     else:
                         lhs, lhs_s = g_codes[:, k, i * P : (i + 1) * P], g_scales[:, k, i * P : (i + 1) * P]
@@ -208,38 +218,46 @@ def tile_classifier_v_kernel(tc, emb, weight, emb_norm, weight_norm, grad_out, o
                         rhs=rhs.bitcast(E4M3), rhs_scale=rhs_s, start=(k == 0), stop=(k == passes - 1),
                     )
 
+        def row_sum(tile, h):
+            if h == 0:
+                res[tile] = stage.tile([P, D], F32, name="wide", bufs=9)
+                sums[tile] = stage.tile([P, 2], F32, name="sums", bufs=4)
+            nc.vector.scalar_tensor_tensor(
+                out=res[tile][:, halves[h]], in0=acc[tile, h][:], scalar=const_of(tile, 0),
+                in1=rows_of(tile)[:, halves[h]], op0=ALU.mult, op1=ALU.mult,
+                accum_out=sums[tile][:, h : h + 1],
+            )
+
         def row_sums(tile):
-            res[tile] = stage.tile([P, D], F32, name="res", bufs=6)
-            sums[tile] = stage.tile([P, 2], F32, name="sums", bufs=4)
-            for h in range(2):
-                nc.vector.scalar_tensor_tensor(
-                    out=res[tile][:, halves[h]], in0=acc[tile, h][:], scalar=const_of(tile, 0),
-                    in1=rows_of(tile)[:, halves[h]], op0=ALU.mult, op1=ALU.mult,
-                    accum_out=sums[tile][:, h : h + 1],
-                )
+            row_sum(tile, 0)
+            row_sum(tile, 1)
 
         def early_coefficient(tile):
             coef[tile] = stage.tile([P, 1], F32, name="coef", bufs=4)
+            parts = stage.tile([P, 2], F32, name="parts", bufs=4)
             nc.vector.tensor_scalar(
-                out=coef[tile][:], in0=sums[tile][:, 0:1], scalar1=sums[tile][:, 1:2],
-                scalar2=e_neg_inv[:, tile[1] : tile[1] + 1], op0=ALU.add, op1=ALU.mult,
+                out=parts[:], in0=sums[tile][:], scalar1=e_neg_inv[:, tile[1] : tile[1] + 1], scalar2=None,
+                op0=ALU.mult, op1=ALU.add, accum_out=coef[tile][:],
             )
 
-        def early_finish(tile):
-            for h in range(2):
-                nc.vector.scalar_tensor_tensor(
-                    out=res[tile][:, halves[h]], in0=rows_of(tile)[:, halves[h]], scalar=coef[tile][:],
-                    in1=acc[tile, h][:], op0=ALU.mult, op1=ALU.add,
-                )
-                nc.gpsimd.tensor_scalar(
-                    out=res[tile][:, halves[h]], in0=res[tile][:, halves[h]], scalar1=const_of(tile, 1),
-                    scalar2=1.0, op0=ALU.mult, op1=ALU.mult,
-                )
+        def early_finish(tile, h):
+            nc.vector.scalar_tensor_tensor(
+                out=res[tile][:, halves[h]], in0=rows_of(tile)[:, halves[h]], scalar=coef[tile][:],
+                in1=acc[tile, h][:], op0=ALU.mult, op1=ALU.add,
+            )
+
+        def gain_gpsimd(tile):
+            nc.gpsimd.tensor_scalar(
+                out=res[tile][:], in0=res[tile][:], scalar1=const_of(tile, 1), scalar2=1.0, op0=ALU.mult, op1=ALU.mult
+            )
+
+        def gain_scalar(tile):
+            nc.scalar.activation(out=res[tile][:], in_=res[tile][:], func=ACT.Copy, scale=const_of(tile, 1))
 
         def late_coefficient(tile):
             coef[tile] = stage.tile([P, 1], F32, name="coef", bufs=4)
-            parts = stage.tile([P, 2], F32, name="parts", bufs=2)
-            term[tile] = stage.tile([P, D], F32, name="term", bufs=3)
+            parts = stage.tile([P, 2], F32, name="parts", bufs=4)
+            term[tile] = stage.tile([P, D], F32, name="wide", bufs=9)
             nc.scalar.activation(
                 out=parts[:], in_=sums[tile][:], func=ACT.Copy, scale=const_of(tile, 2), accum_out=coef[tile][:]
             )
@@ -273,23 +291,25 @@ def tile_classifier_v_kernel(tc, emb, weight, emb_norm, weight_norm, grad_out, o
         w_inv = inverse(w_norm[:].rearrange("p q j -> p (q j)"), CLASS_PASSES * PACK, "w_inv")
 
         def w_normalise(q, h):
-            normalise(("w", q, h), w_raw[q, h], w_inv, q * PACK, range(PACK))
+            if h == 0:
+                unit["w", q] = stage.tile([P, 2, PACK, HALF], BF16, name="unit", bufs=2, align_bytes=64)
+            normalise(unit["w", q][:, h, :, :], w_raw[q, h], w_inv, q * PACK)
 
-        def w_interleave(q, h, on_vector):
-            interleave(("w", q, h), unit["w", q, h][:], on_vector)
+        def w_interleave(q, h, engine):
+            interleave(("w", q), unit["w", q][:, h, :, :], halves[h], engine)
 
         def w_quantise(q, h):
-            quantise(("w", q, h), w_codes[:, q, halves[h]], w_scales[:, q, halves[h]], E4M3)
+            quantise(("w", q), halves[h], w_codes[:, q, :], w_scales[:, q, :], E4M3)
 
         w_normalise(0, 0)
-        w_interleave(0, 0, False)
+        w_interleave(0, 0, "scalar")
         e_inv = inverse(e_norm[:].rearrange("p g j -> p (g j)"), N // P, "e_inv")
         w_normalise(1, 0)
         consts["emb"] = row_constants(e_inv, N // P, "emb")
         e_neg_inv = negated(e_inv, N // P)
         w_normalise(0, 1)
-        w_interleave(0, 1, False)
-        w_interleave(1, 0, True)
+        w_interleave(0, 1, "scalar")
+        w_interleave(1, 0, "vector")
         transpose_pair(0)
         transpose_pair(1)
         copy_pair(0)
@@ -297,129 +317,123 @@ def tile_classifier_v_kernel(tc, emb, weight, emb_norm, weight_norm, grad_out, o
         w_quantise(1, 0)
         w_normalise(1, 1)
         w_quantise(0, 1)
-        w_interleave(1, 1, True)
-        quantise_pair(0)
+        w_interleave(1, 1, "vector")
+        quantise_flipped(0, slice(0, 2))
         w_quantise(1, 1)
 
-        early = TOKEN_PASSES * STEPS_PER_PASS
-        order = [("emb", i) for i in range(early)]
-        for i in range(early, N // P):
-            m = 2 * (i - early)
-            order.extend([("emb", i), ("w", m), ("w", m + 1)])
+        whole = slice(0, D)
 
-        def g_interleave(g, h):
-            interleave(("g", g, h), g_raw[g][:, :, halves[h]], False)
+        def g_quantise(g):
+            quantise(("g", g), whole, g_codes[:, g, :], g_scales[:, g, :], E5M2)
 
-        def e_interleave(g, h):
-            interleave(("e", g, h), unit["e", g][:, :, halves[h]], False)
+        def e_quantise(g):
+            quantise(("e", g), whole, e_codes[:, g, :], e_scales[:, g, :], E4M3)
 
-        def g_quantise(g, h):
-            quantise(("g", g, h), g_codes[:, g, halves[h]], g_scales[:, g, halves[h]], E5M2)
+        early = sum(WINDOW_TILES)
+        late = [("emb", early)]
+        for m in range(A // P):
+            if early + 1 + m < N // P:
+                late.append(("emb", early + 1 + m))
+            late.append(("w", m))
 
-        def e_quantise(g, h):
-            quantise(("e", g, h), e_codes[:, g, halves[h]], e_scales[:, g, halves[h]], E4M3)
+        waiting = []
+        done = 0
+        for g in range(TOKEN_PASSES):
+            last = g + 1 == TOKEN_PASSES
+            tiles = [("emb", done + t) for t in range(WINDOW_TILES[g])]
+            done = done + len(tiles)
+            if g > 0:
+                quantise_flipped(g, slice(0, PACK))
+                g_quantise(g - 1)
+                e_quantise(g - 1)
+            if g == 2:
+                row_inv = inverse(row_norm[:], A // P, "row_inv")
+            if g == 3:
+                consts["w"] = row_constants(row_inv, A // P, "w")
+            if g == 0:
+                copy_pair(1)
+                quantise_flipped(0, slice(2, PACK))
+            unit["e", g] = stage.tile([P, PACK, D], BF16, name="unit", bufs=2, align_bytes=64)
+            normalise(unit["e", g], e_raw[g], e_inv, g * PACK)
 
-        def e_normalise(g, slots):
-            normalise(("e", g), e_raw[g], consts["emb"][0], g * PACK, slots)
+            split = GPSIMD_COLS[g]
+            interleave(("e", g), unit["e", g][:, :, 0:split], slice(0, split), "gpsimd")
+            for tile in waiting:
+                gain_gpsimd(tile)
+                store(tile)
+            for h in range(2):
+                interleave(("g", g), g_raw[g][:, :, halves[h]], halves[h], "scalar")
+            if g == 0:
+                load_g(TOKEN_PASSES - 1)
+            if g == 1:
+                for s in range(A // P // 2):
+                    load_w_rows(s)
 
-        def vector_chunk(step):
-            g, part = divmod(step, STEPS_PER_PASS)
-            calls = []
-            if part == 0:
-                if g > 0:
-                    calls.append(lambda: e_quantise(g - 1, 0))
-                if g < TOKEN_PASSES:
-                    calls.append(lambda: e_normalise(g, range(PACK)))
-                    if g > 0:
-                        calls.append(lambda: quantise_pair(2 * g + 1))
-                else:
-                    calls.append(lambda: e_quantise(g - 1, 1))
-            elif part == 1:
-                if g > 0:
-                    calls.append(lambda: e_quantise(g - 1, 1))
-                else:
-                    calls.append(lambda: quantise_pair(1))
-                calls.append(lambda: g_quantise(g, 0))
+            multiply(tiles[0])
+            multiply(tiles[1])
+            if not last:
+                transpose_pair(2 * g + 2)
+            for tile in tiles[2:]:
+                multiply(tile)
+                copy_pair(2 * g + 2)
+            if not last:
+                transpose_pair(2 * g + 3)
+                if len(tiles) == 2:
+                    copy_pair(2 * g + 2)
+                copy_pair(2 * g + 3)
             else:
-                calls.append(lambda: g_quantise(g, 1))
-                if g + 1 < TOKEN_PASSES:
-                    calls.append(lambda: quantise_pair(2 * g + 2))
-            return calls
+                multiply(late[0])
+                multiply(("w", 0), upto=TOKEN_PASSES - 1)
+            if split < D:
+                interleave(("e", g), unit["e", g][:, :, split:D], slice(split, D), "scalar")
+
+            row_sums(tiles[0])
+            for t in range(1, len(tiles)):
+                row_sum(tiles[t], 0)
+                early_coefficient(tiles[t - 1])
+                row_sum(tiles[t], 1)
+                early_finish(tiles[t - 1], 0)
+                if t + 1 == len(tiles):
+                    early_coefficient(tiles[t])
+                early_finish(tiles[t - 1], 1)
+            early_finish(tiles[-1], 0)
+            early_finish(tiles[-1], 1)
+            waiting = tiles
 
         def late_start(tile):
             late_coefficient(tile)
             scale_scalar(tile)
-            term_scalar(tile, slice(0, D))
+            term_scalar(tile, whole)
             finish_gpsimd(tile)
 
-        busy = early - 1
-        multiply(order[0])
-        for step in range(early + 1):
-            g, part = divmod(step, STEPS_PER_PASS)
-            last = g + 1 >= TOKEN_PASSES
-            chunk = vector_chunk(step)
-            finish_early = 0 < step <= busy
-            if finish_early and len(chunk) == 1:
-                early_coefficient(order[step - 1])
-            chunk[0]()
-            if finish_early and len(chunk) > 1:
-                early_coefficient(order[step - 1])
-            for call in chunk[1:]:
-                call()
-            if part == 0 and g < TOKEN_PASSES:
-                g_interleave(g, 0)
-            if step == 0:
-                copy_pair(1)
-            if part == 1:
-                g_interleave(g, 1)
-            multiply(order[step + 1])
-            if part == 0 and not last:
-                transpose_pair(2 * g + 2)
-            if part == 1:
-                if not last:
-                    copy_pair(2 * g + 2)
-                    transpose_pair(2 * g + 3)
-                e_interleave(g, 0)
-            if part == 2:
-                if not last:
-                    copy_pair(2 * g + 3)
-                else:
-                    multiply(("w", 0), upto=TOKEN_PASSES - 1)
-                e_interleave(g, 1)
-            if finish_early:
-                early_finish(order[step - 1])
-                store(order[step - 1])
-            row_sums(order[step])
-            if step >= busy:
-                late_start(order[step])
-            if step == 1:
-                load_g(TOKEN_PASSES - 1)
-            if 4 <= step < 8:
-                load_w_rows(step - 4)
-            if step == 7:
-                row_inv = inverse(row_norm[:], A // P, "row_inv")
-            if step == 8:
-                consts["w"] = row_constants(row_inv, A // P, "w")
+        multiply(late[1])
+        g_quantise(TOKEN_PASSES - 1)
+        row_sums(late[0])
+        e_quantise(TOKEN_PASSES - 1)
+        for tile in waiting:
+            gain_scalar(tile)
+            store(tile)
+        late_start(late[0])
 
-        final = len(order) - 1
-        store(order[busy], halves[1])
-        for step in range(early + 1, final):
-            multiply(order[step + 1])
-            row_sums(order[step])
-            late_start(order[step])
-            finish_vector(order[step - 2], 0)
-            store(order[step - 2], halves[0])
-            store(order[step - 1], halves[1])
-        tile = order[final]
+        final = len(late) - 1
+        for step in range(1, final):
+            multiply(late[step + 1])
+            row_sums(late[step])
+            late_start(late[step])
+            if step >= 2:
+                finish_vector(late[step - 2], 0)
+                store(late[step - 2], halves[0])
+            store(late[step - 1], halves[1])
+        tile = late[final]
         row_sums(tile)
         late_coefficient(tile)
         term_scalar(tile, halves[0])
         term_scalar(tile, halves[1])
-        finish_vector(order[final - 2], 0)
-        store(order[final - 2], halves[0])
-        finish_vector(order[final - 1], 0)
+        finish_vector(late[final - 2], 0)
+        store(late[final - 2], halves[0])
+        finish_vector(late[final - 1], 0)
         for h in range(2):
-            store(order[final - 1], halves[h])
+            store(late[final - 1], halves[h])
         for h in range(2):
             finish_vector(tile, h)
             store(tile, halves[h])

@@ -22,8 +22,8 @@ HALF = 512
 TOKEN_PASSES = N // KP
 CLASS_PASSES = A // KP
 FACTOR = 10.0
-WINDOW_TILES = (3, 2, 2, 2)
-GPSIMD_COLS = (1024, 64, 320, 320)
+WINDOW_TILES = (3, 3, 2, 2)
+GPSIMD_COLS = (768, 320, 64, 192)
 
 
 def tile_classifier_v_kernel(tc, emb, weight, emb_norm, weight_norm, grad_out, out_0, out_1):
@@ -80,14 +80,14 @@ def tile_classifier_v_kernel(tc, emb, weight, emb_norm, weight_norm, grad_out, o
         ident = keep.tile([P, P], F32)
         make_identity(nc, ident[:])
 
-        w_codes = keep.tile([P, CLASS_PASSES, D], U32, align_bytes=64)
-        w_scales = keep.tile([P, CLASS_PASSES, D], U8, align_bytes=64)
-        gt_codes = keep.tile([P, TOKEN_PASSES, PACK, CLASS_PASSES * P], U32, align_bytes=64)
-        gt_scales = keep.tile([P, TOKEN_PASSES, PACK, CLASS_PASSES * P], U8, align_bytes=64)
-        g_codes = keep.tile([P, TOKEN_PASSES, A], U32, align_bytes=64)
-        g_scales = keep.tile([P, TOKEN_PASSES, A], U8, align_bytes=64)
-        e_codes = keep.tile([P, TOKEN_PASSES, D], U32, align_bytes=64)
-        e_scales = keep.tile([P, TOKEN_PASSES, D], U8, align_bytes=64)
+        w_codes = keep.tile([P, CLASS_PASSES, D], U32, align_bytes=256)
+        w_scales = keep.tile([P, CLASS_PASSES, D], U8, align_bytes=256)
+        gt_codes = keep.tile([P, TOKEN_PASSES, PACK, CLASS_PASSES * P], U32, align_bytes=256)
+        gt_scales = keep.tile([P, TOKEN_PASSES, PACK, CLASS_PASSES * P], U8, align_bytes=256)
+        g_codes = keep.tile([P, TOKEN_PASSES, A], U32, align_bytes=256)
+        g_scales = keep.tile([P, TOKEN_PASSES, A], U8, align_bytes=256)
+        e_codes = keep.tile([P, TOKEN_PASSES, D], U32, align_bytes=256)
+        e_scales = keep.tile([P, TOKEN_PASSES, D], U8, align_bytes=256)
 
         def inverse(norm, width, name):
             inv = keep.tile([P, width], F32, name=name)
@@ -330,11 +330,13 @@ def tile_classifier_v_kernel(tc, emb, weight, emb_norm, weight_norm, grad_out, o
             quantise(("e", g), whole, e_codes[:, g, :], e_scales[:, g, :], E4M3)
 
         early = sum(WINDOW_TILES)
-        late = [("emb", early)]
-        for m in range(A // P):
-            if early + 1 + m < N // P:
-                late.append(("emb", early + 1 + m))
+        late = [("emb", early), ("emb", early + 1), ("w", 0), ("w", 1)]
+        rest = list(range(early + 2, N // P))
+        for m in range(2, A // P):
             late.append(("w", m))
+            behind = A // P - 1 - m
+            if behind < len(rest):
+                late.append(("emb", rest[len(rest) - 1 - behind]))
 
         waiting = []
         done = 0
@@ -382,8 +384,8 @@ def tile_classifier_v_kernel(tc, emb, weight, emb_norm, weight_norm, grad_out, o
                     copy_pair(2 * g + 2)
                 copy_pair(2 * g + 3)
             else:
-                multiply(late[0])
                 multiply(("w", 0), upto=TOKEN_PASSES - 1)
+                multiply(("w", 1), upto=TOKEN_PASSES - 1)
             if split < D:
                 interleave(("e", g), unit["e", g][:, :, split:D], slice(split, D), "scalar")
 
@@ -396,6 +398,8 @@ def tile_classifier_v_kernel(tc, emb, weight, emb_norm, weight_norm, grad_out, o
                 if t + 1 == len(tiles):
                     early_coefficient(tiles[t])
                 early_finish(tiles[t - 1], 1)
+            if last:
+                multiply(late[0])
             early_finish(tiles[-1], 0)
             early_finish(tiles[-1], 1)
             waiting = tiles

@@ -22,8 +22,8 @@ HALF = 512
 TOKEN_PASSES = N // KP
 CLASS_PASSES = A // KP
 FACTOR = 10.0
-WINDOW_TILES = (3, 3, 2, 2)
-GPSIMD_COLS = (768, 320, 64, 192)
+WINDOW_TILES = (2, 2, 2, 2)
+GPSIMD_COLS = (704, 320, 320, 320)
 
 
 def tile_classifier_v_kernel(tc, emb, weight, emb_norm, weight_norm, grad_out, out_0, out_1):
@@ -82,8 +82,8 @@ def tile_classifier_v_kernel(tc, emb, weight, emb_norm, weight_norm, grad_out, o
 
         w_codes = keep.tile([P, CLASS_PASSES, D], U32, align_bytes=256)
         w_scales = keep.tile([P, CLASS_PASSES, D], U8, align_bytes=256)
-        gt_codes = keep.tile([P, TOKEN_PASSES, PACK, CLASS_PASSES * P], U32, align_bytes=256)
-        gt_scales = keep.tile([P, TOKEN_PASSES, PACK, CLASS_PASSES * P], U8, align_bytes=256)
+        gt_codes = keep.tile([P, N // P, CLASS_PASSES * P], U32, align_bytes=256)
+        gt_scales = keep.tile([P, N // P, CLASS_PASSES * P], U8, align_bytes=256)
         g_codes = keep.tile([P, TOKEN_PASSES, A], U32, align_bytes=256)
         g_scales = keep.tile([P, TOKEN_PASSES, A], U8, align_bytes=256)
         e_codes = keep.tile([P, TOKEN_PASSES, D], U32, align_bytes=256)
@@ -99,14 +99,9 @@ def tile_classifier_v_kernel(tc, emb, weight, emb_norm, weight_norm, grad_out, o
             pull = keep.tile([P, width], F32, name=name + "_pull")
             nc.vector.tensor_scalar(out=gain[:], in0=inv[:], scalar1=FACTOR, scalar2=None, op0=ALU.mult)
             nc.vector.scalar_tensor_tensor(
-                out=pull[:], in0=inv[:], scalar=-FACTOR, in1=inv[:], op0=ALU.mult, op1=ALU.mult
+                out=pull[:], in0=inv[:], scalar=-1.0, in1=inv[:], op0=ALU.mult, op1=ALU.mult
             )
-            return inv, gain, pull
-
-        def negated(inv, width):
-            neg = keep.tile([P, width], F32)
-            nc.vector.tensor_scalar(out=neg[:], in0=inv[:], scalar1=-1.0, scalar2=None, op0=ALU.mult)
-            return neg
+            return pull, gain
 
         unit = {}
         grouped = {}
@@ -155,21 +150,20 @@ def tile_classifier_v_kernel(tc, emb, weight, emb_norm, weight_norm, grad_out, o
                             tr_bank[i][:, col : col + P], words[:, 256 * q + u : 256 * (q + 1) : 2], ident[:]
                         )
 
-        def copy_pair(pair):
-            g = pair // 2
-            if g not in flipped:
-                flipped[g] = stage.tile([P, PACK, A], BF16, name="flipped", bufs=1, align_bytes=64)
-            for i in (2 * pair, 2 * pair + 1):
+        def copy_pair(pair, batch, slot):
+            if batch not in flipped:
+                flipped[batch] = stage.tile([P, PACK, A], BF16, name="flipped", bufs=1, align_bytes=64)
+            for s in range(2):
                 nc.scalar.copy(
-                    out=flipped[g][:, i % PACK, :].bitcast(F32).rearrange("p (q r u) -> p q r u", q=CLASS_PASSES, u=2),
-                    in_=tr_bank[i][:].rearrange("p (q u r) -> p q r u", q=CLASS_PASSES, u=2),
+                    out=flipped[batch][:, slot + s, :].bitcast(F32).rearrange("p (q r u) -> p q r u", q=CLASS_PASSES, u=2),
+                    in_=tr_bank[2 * pair + s][:].rearrange("p (q u r) -> p q r u", q=CLASS_PASSES, u=2),
                 )
 
-        def quantise_flipped(g, slots):
+        def quantise_flipped(batch, first, count):
             nc.vector.quantize_mx(
-                out=gt_codes[:, g, slots, :].rearrange("p j c -> p (j c)").bitcast(E5M2),
-                scales=gt_scales[:, g, slots, :].rearrange("p j c -> p (j c)"),
-                in_=flipped[g][:, slots, :].rearrange("p j a -> p (j a)"),
+                out=gt_codes[:, first : first + count, :].rearrange("p j c -> p (j c)").bitcast(E5M2),
+                scales=gt_scales[:, first : first + count, :].rearrange("p j c -> p (j c)"),
+                in_=flipped[batch][:, 0:count, :].rearrange("p j a -> p (j a)"),
             )
 
         w_rows = {}
@@ -207,8 +201,7 @@ def tile_classifier_v_kernel(tc, emb, weight, emb_norm, weight_norm, grad_out, o
                     acc[tile, h] = psum.tile([P, HALF], F32, name="bank")
                 for k in range(first, begun[tile]):
                     if kind == "emb":
-                        g, j = divmod(i, PACK)
-                        lhs, lhs_s = gt_codes[:, g, j, k * P : (k + 1) * P], gt_scales[:, g, j, k * P : (k + 1) * P]
+                        lhs, lhs_s = gt_codes[:, i, k * P : (k + 1) * P], gt_scales[:, i, k * P : (k + 1) * P]
                         rhs, rhs_s = w_codes[:, k, halves[h]], w_scales[:, k, halves[h]]
                     else:
                         lhs, lhs_s = g_codes[:, k, i * P : (i + 1) * P], g_scales[:, k, i * P : (i + 1) * P]
@@ -234,11 +227,7 @@ def tile_classifier_v_kernel(tc, emb, weight, emb_norm, weight_norm, grad_out, o
 
         def early_coefficient(tile):
             coef[tile] = stage.tile([P, 1], F32, name="coef", bufs=4)
-            parts = stage.tile([P, 2], F32, name="parts", bufs=4)
-            nc.vector.tensor_scalar(
-                out=parts[:], in0=sums[tile][:], scalar1=e_neg_inv[:, tile[1] : tile[1] + 1], scalar2=None,
-                op0=ALU.mult, op1=ALU.add, accum_out=coef[tile][:],
-            )
+            nc.vector.tensor_reduce(out=coef[tile][:], in_=sums[tile][:], axis=mybir.AxisListType.X, op=ALU.add)
 
         def early_finish(tile, h):
             nc.vector.scalar_tensor_tensor(
@@ -259,7 +248,7 @@ def tile_classifier_v_kernel(tc, emb, weight, emb_norm, weight_norm, grad_out, o
             parts = stage.tile([P, 2], F32, name="parts", bufs=4)
             term[tile] = stage.tile([P, D], F32, name="wide", bufs=9)
             nc.scalar.activation(
-                out=parts[:], in_=sums[tile][:], func=ACT.Copy, scale=const_of(tile, 2), accum_out=coef[tile][:]
+                out=parts[:], in_=sums[tile][:], func=ACT.Copy, scale=const_of(tile, 1), accum_out=coef[tile][:]
             )
 
         def term_scalar(tile, cols):
@@ -306,19 +295,17 @@ def tile_classifier_v_kernel(tc, emb, weight, emb_norm, weight_norm, grad_out, o
         e_inv = inverse(e_norm[:].rearrange("p g j -> p (g j)"), N // P, "e_inv")
         w_normalise(1, 0)
         consts["emb"] = row_constants(e_inv, N // P, "emb")
-        e_neg_inv = negated(e_inv, N // P)
         w_normalise(0, 1)
         w_interleave(0, 1, "scalar")
         w_interleave(1, 0, "vector")
         transpose_pair(0)
-        transpose_pair(1)
-        copy_pair(0)
+        copy_pair(0, "head", 0)
         w_quantise(0, 0)
         w_quantise(1, 0)
         w_normalise(1, 1)
         w_quantise(0, 1)
         w_interleave(1, 1, "vector")
-        quantise_flipped(0, slice(0, 2))
+        quantise_flipped("head", 0, 2)
         w_quantise(1, 1)
 
         whole = slice(0, D)
@@ -345,16 +332,13 @@ def tile_classifier_v_kernel(tc, emb, weight, emb_norm, weight_norm, grad_out, o
             tiles = [("emb", done + t) for t in range(WINDOW_TILES[g])]
             done = done + len(tiles)
             if g > 0:
-                quantise_flipped(g, slice(0, PACK))
+                quantise_flipped(g - 1, PACK * g - 2, PACK)
                 g_quantise(g - 1)
                 e_quantise(g - 1)
             if g == 2:
                 row_inv = inverse(row_norm[:], A // P, "row_inv")
             if g == 3:
                 consts["w"] = row_constants(row_inv, A // P, "w")
-            if g == 0:
-                copy_pair(1)
-                quantise_flipped(0, slice(2, PACK))
             unit["e", g] = stage.tile([P, PACK, D], BF16, name="unit", bufs=2, align_bytes=64)
             normalise(unit["e", g], e_raw[g], e_inv, g * PACK)
 
@@ -365,27 +349,23 @@ def tile_classifier_v_kernel(tc, emb, weight, emb_norm, weight_norm, grad_out, o
                 store(tile)
             for h in range(2):
                 interleave(("g", g), g_raw[g][:, :, halves[h]], halves[h], "scalar")
-            if g == 0:
-                load_g(TOKEN_PASSES - 1)
             if g == 1:
                 for s in range(A // P // 2):
                     load_w_rows(s)
 
             multiply(tiles[0])
             multiply(tiles[1])
-            if not last:
-                transpose_pair(2 * g + 2)
-            for tile in tiles[2:]:
-                multiply(tile)
-                copy_pair(2 * g + 2)
-            if not last:
-                transpose_pair(2 * g + 3)
-                if len(tiles) == 2:
-                    copy_pair(2 * g + 2)
-                copy_pair(2 * g + 3)
-            else:
+            transpose_pair(2 * g + 1)
+            if last:
                 multiply(("w", 0), upto=TOKEN_PASSES - 1)
+                copy_pair(2 * g + 1, g, 0)
                 multiply(("w", 1), upto=TOKEN_PASSES - 1)
+            else:
+                transpose_pair(2 * g + 2)
+                copy_pair(2 * g + 1, g, 0)
+                copy_pair(2 * g + 2, g, 2)
+            if g == 0:
+                load_g(TOKEN_PASSES - 1)
             if split < D:
                 interleave(("e", g), unit["e", g][:, :, split:D], slice(split, D), "scalar")
 
@@ -411,6 +391,7 @@ def tile_classifier_v_kernel(tc, emb, weight, emb_norm, weight_norm, grad_out, o
             finish_gpsimd(tile)
 
         multiply(late[1])
+        quantise_flipped(TOKEN_PASSES - 1, N // P - 2, 2)
         g_quantise(TOKEN_PASSES - 1)
         row_sums(late[0])
         e_quantise(TOKEN_PASSES - 1)

from contextlib import ExitStack

import concourse.mybir as mybir
from concourse.masks import make_identity

N, A, D = 2048, 1024, 1024
FLOPS = 2 * 2 * N * A * D

F32 = mybir.dt.float32
BF16 = mybir.dt.bfloat16
U32 = mybir.dt.uint32
U8 = mybir.dt.uint8
E4M3 = mybir.dt.float8_e4m3fn_x4
E5M2 = mybir.dt.float8_e5m2_x4
ALU = mybir.AluOpType
ACT = mybir.ActivationFunctionType

P = 128
PACK = 4
KP = P * PACK
HALF = 512
TOKEN_PASSES = N // KP
CLASS_PASSES = A // KP
FACTOR = 10.0
WINDOW_TILES = (2, 2, 2, 2)
GPSIMD_COLS = (704, 320, 320, 320)


def tile_classifier_v_kernel(tc, emb, weight, emb_norm, weight_norm, grad_out, out_0, out_1):
    nc = tc.nc
    halves = [slice(0, HALF), slice(HALF, D)]

    with ExitStack() as ctx:
        keep = ctx.enter_context(tc.tile_pool(name="keep", bufs=1))
        stage = ctx.enter_context(tc.tile_pool(name="stage", bufs=2))
        psum = ctx.enter_context(tc.psum_pool(name="psum", bufs=8))
        ctx.enter_context(tc.manual_schedule())

        emb_v = emb.rearrange("(g p j) d -> g p j d", p=P, j=PACK)
        grad_v = grad_out.rearrange("(g p j) a -> g p j a", p=P, j=PACK)
        w_v = weight.rearrange("(q p j) d -> q p j d", p=P, j=PACK)
        w_rows_v = weight.rearrange("(s t p) d -> s p t d", p=P, t=2)
        out0_v = out_0.rearrange("(g p j) d -> g j p d", p=P, j=PACK)
        out1_v = out_1.rearrange("(t p) d -> t p d", p=P)

        w_norm = keep.tile([P, CLASS_PASSES, PACK], F32)
        nc.scalar.dma_start(out=w_norm[:], in_=weight_norm.rearrange("(q p j) o -> p q (j o)", p=P, j=PACK))
        e_norm = keep.tile([P, TOKEN_PASSES, PACK], F32)
        nc.scalar.dma_start(out=e_norm[:], in_=emb_norm.rearrange("(g p j) o -> p g (j o)", p=P, j=PACK))
        w_raw = {}
        g_raw = {}
        e_raw = {}

        def load_w(q, h):
            w_raw[q, h] = stage.tile([P, PACK, HALF], BF16, name="w_raw", bufs=4, align_bytes=64)
            nc.sync.dma_start(out=w_raw[q, h][:], in_=w_v[q][:, :, halves[h]])

        def load_g(g):
            g_raw[g] = stage.tile([P, PACK, A], BF16, name="g_raw", bufs=3, align_bytes=64)
            nc.sync.dma_start(out=g_raw[g][:], in_=grad_v[g])

        def load_e(g):
            e_raw[g] = stage.tile([P, PACK, D], BF16, name="e_raw", bufs=4, align_bytes=64)
            nc.sync.dma_start(out=e_raw[g][:], in_=emb_v[g])

        load_w(0, 0)
        load_w(1, 0)
        load_w(0, 1)
        load_g(0)
        load_w(1, 1)
        load_e(0)
        for g in range(1, TOKEN_PASSES):
            if g + 1 < TOKEN_PASSES:
                load_g(g)
            load_e(g)
        row_norm = keep.tile([P, A // P], F32)
        with nc.allow_non_contiguous_dma(reason="one norm for each partition and class tile"):
            nc.sync.dma_start(out=row_norm[:], in_=weight_norm.rearrange("(t p) o -> p (t o)", p=P))

        ident = keep.tile([P, P], F32)
        make_identity(nc, ident[:])

        w_codes = keep.tile([P, CLASS_PASSES, D], U32, align_bytes=256)
        w_scales = keep.tile([P, CLASS_PASSES, D], U8, align_bytes=256)
        gt_codes = keep.tile([P, N // P, CLASS_PASSES * P], U32, align_bytes=256)
        gt_scales = keep.tile([P, N // P, CLASS_PASSES * P], U8, align_bytes=256)
        g_codes = keep.tile([P, TOKEN_PASSES, A], U32, align_bytes=256)
        g_scales = keep.tile([P, TOKEN_PASSES, A], U8, align_bytes=256)
        e_codes = keep.tile([P, TOKEN_PASSES, D], U32, align_bytes=256)
        e_scales = keep.tile([P, TOKEN_PASSES, D], U8, align_bytes=256)

        def inverse(norm, width, name):
            inv = keep.tile([P, width], F32, name=name)
            nc.vector.reciprocal(out=inv[:], in_=norm)
            return inv

        def row_constants(inv, width, name):
            gain = keep.tile([P, width], F32, name=name + "_gain")
            pull = keep.tile([P, width], F32, name=name + "_pull")
            nc.vector.tensor_scalar(out=gain[:], in0=inv[:], scalar1=FACTOR, scalar2=None, op0=ALU.mult)
            nc.vector.scalar_tensor_tensor(
                out=pull[:], in0=inv[:], scalar=-1.0, in1=inv[:], op0=ALU.mult, op1=ALU.mult
            )
            return pull, gain

        unit = {}
        grouped = {}
        flipped = {}

        def normalise(dst, raw, inv, first):
            for j in range(PACK):
                nc.vector.tensor_scalar(
                    out=dst[:, j, :], in0=raw[:, j, :], scalar1=inv[:, first + j : first + j + 1],
                    scalar2=None, op0=ALU.mult,
                )

        def interleave(key, src, cols, engine):
            if key not in grouped:
                grouped[key] = stage.tile([P, D, PACK], BF16, name="grouped", bufs=4, align_bytes=64)
            if engine == "gpsimd":
                nc.gpsimd.tensor_scalar(
                    out=grouped[key][:, cols, :], in0=src.rearrange("p j c -> p c j"),
                    scalar1=1.0, scalar2=0.0, op0=ALU.mult, op1=ALU.add,
                )
                return
            dst_v = grouped[key][:, cols, :].rearrange("p (c i) j -> p c j i", i=4)
            src_v = src.rearrange("p j (c i) -> p c j i", i=4)
            if engine == "vector":
                nc.vector.tensor_copy(out=dst_v, in_=src_v)
            else:
                nc.scalar.copy(out=dst_v, in_=src_v)

        def quantise(key, cols, codes, scales, fmt):
            nc.vector.quantize_mx(
                out=codes[:, cols].bitcast(fmt), scales=scales[:, cols],
                in_=grouped[key][:, cols, :].rearrange("p c j -> p (c j)"),
            )

        tr_bank = {}

        def transpose_pair(pair):
            for i in (2 * pair, 2 * pair + 1):
                g, j = divmod(i, PACK)
                words = g_raw[g][:, j, :].bitcast(F32)
                tr_bank[i] = psum.tile([P, HALF], F32, name="bank")
                for q in range(CLASS_PASSES):
                    for u in range(2):
                        col = (2 * q + u) * P
                        nc.tensor.transpose(
                            tr_bank[i][:, col : col + P], words[:, 256 * q + u : 256 * (q + 1) : 2], ident[:]
                        )

        def copy_pair(pair, batch, slot):
            if batch not in flipped:
                flipped[batch] = stage.tile([P, PACK, A], BF16, name="flipped", bufs=1, align_bytes=64)
            for s in range(2):
                nc.scalar.copy(
                    out=flipped[batch][:, slot + s, :].bitcast(F32).rearrange("p (q r u) -> p q r u", q=CLASS_PASSES, u=2),
                    in_=tr_bank[2 * pair + s][:].rearrange("p (q u r) -> p q r u", q=CLASS_PASSES, u=2),
                )

        def quantise_flipped(batch, first, count):
            nc.vector.quantize_mx(
                out=gt_codes[:, first : first + count, :].rearrange("p j c -> p (j c)").bitcast(E5M2),
                scales=gt_scales[:, first : first + count, :].rearrange("p j c -> p (j c)"),
                in_=flipped[batch][:, 0:count, :].rearrange("p j a -> p (j a)"),
            )

        w_rows = {}

        def load_w_rows(s):
            w_rows[s] = stage.tile([P, 2, D], BF16, name="w_raw", bufs=4, align_bytes=64)
            nc.sync.dma_start(out=w_rows[s][:], in_=w_rows_v[s])

        acc = {}
        res = {}
        sums = {}
        coef = {}
        term = {}
        consts = {}

        def rows_of(tile):
            kind, i = tile
            if kind == "emb":
                return e_raw[i // PACK][:, i % PACK, :]
            return w_rows[i // 2][:, i % 2, :]

        def const_of(tile, which):
            kind, i = tile
            return consts[kind][which][:, i : i + 1]

        begun = {}

        def multiply(tile, upto=None):
            kind, i = tile
            passes = CLASS_PASSES if kind == "emb" else TOKEN_PASSES
            first = begun.get(tile, 0)
            begun[tile] = passes if upto is None else upto
            for h in range(2):
                if first == 0:
                    acc[tile, h] = psum.tile([P, HALF], F32, name="bank")
                for k in range(first, begun[tile]):
                    if kind == "emb":
                        lhs, lhs_s = gt_codes[:, i, k * P : (k + 1) * P], gt_scales[:, i, k * P : (k + 1) * P]
                        rhs, rhs_s = w_codes[:, k, halves[h]], w_scales[:, k, halves[h]]
                    else:
                        lhs, lhs_s = g_codes[:, k, i * P : (i + 1) * P], g_scales[:, k, i * P : (i + 1) * P]
                        rhs, rhs_s = e_codes[:, k, halves[h]], e_scales[:, k, halves[h]]
                    nc.tensor.matmul_mx(
                        out=acc[tile, h][:], lhsT=lhs.bitcast(E5M2), lhsT_scale=lhs_s,
                        rhs=rhs.bitcast(E4M3), rhs_scale=rhs_s, start=(k == 0), stop=(k == passes - 1),
                    )

        def row_sum(tile, h):
            if h == 0:
                res[tile] = stage.tile([P, D], F32, name="wide", bufs=9)
                sums[tile] = stage.tile([P, 2], F32, name="sums", bufs=4)
            nc.vector.scalar_tensor_tensor(
                out=res[tile][:, halves[h]], in0=acc[tile, h][:], scalar=const_of(tile, 0),
                in1=rows_of(tile)[:, halves[h]], op0=ALU.mult, op1=ALU.mult,
                accum_out=sums[tile][:, h : h + 1],
            )

        def row_sums(tile):
            row_sum(tile, 0)
            row_sum(tile, 1)

        def early_coefficient(tile):
            coef[tile] = stage.tile([P, 1], F32, name="coef", bufs=4)
            nc.vector.tensor_reduce(out=coef[tile][:], in_=sums[tile][:], axis=mybir.AxisListType.X, op=ALU.add)

        def early_finish(tile, h):
            nc.vector.scalar_tensor_tensor(
                out=res[tile][:, halves[h]], in0=rows_of(tile)[:, halves[h]], scalar=coef[tile][:],
                in1=acc[tile, h][:], op0=ALU.mult, op1=ALU.add,
            )

        def gain_gpsimd(tile):
            nc.gpsimd.tensor_scalar(
                out=res[tile][:], in0=res[tile][:], scalar1=const_of(tile, 1), scalar2=1.0, op0=ALU.mult, op1=ALU.mult
            )

        def gain_scalar(tile):
            nc.scalar.activation(out=res[tile][:], in_=res[tile][:], func=ACT.Copy, scale=const_of(tile, 1))

        def late_coefficient(tile):
            coef[tile] = stage.tile([P, 1], F32, name="coef", bufs=4)
            parts = stage.tile([P, 2], F32, name="parts", bufs=4)
            term[tile] = stage.tile([P, D], F32, name="wide", bufs=9)
            nc.scalar.activation(
                out=parts[:], in_=sums[tile][:], func=ACT.Copy, scale=const_of(tile, 1), accum_out=coef[tile][:]
            )

        def term_scalar(tile, cols):
            nc.scalar.activation(
                out=term[tile][:, cols], in_=rows_of(tile)[:, cols], func=ACT.Copy, scale=coef[tile][:]
            )

        def finish_vector(tile, h):
            nc.vector.scalar_tensor_tensor(
                out=res[tile][:, halves[h]], in0=acc[tile, h][:], scalar=const_of(tile, 1),
                in1=term[tile][:, halves[h]], op0=ALU.mult, op1=ALU.add,
            )

        def scale_scalar(tile):
            nc.scalar.activation(
                out=res[tile][:, halves[1]], in_=acc[tile, 1][:], func=ACT.Copy, scale=const_of(tile, 1)
            )

        def finish_gpsimd(tile):
            nc.gpsimd.tensor_tensor(
                out=res[tile][:, halves[1]], in0=res[tile][:, halves[1]], in1=term[tile][:, halves[1]], op=ALU.add
            )

        def store(tile, cols=slice(0, D)):
            kind, i = tile
            dst = out0_v[i // PACK][i % PACK] if kind == "emb" else out1_v[i]
            nc.sync.dma_start(out=dst[:, cols], in_=res[tile][:, cols])

        w_inv = inverse(w_norm[:].rearrange("p q j -> p (q j)"), CLASS_PASSES * PACK, "w_inv")

        def w_normalise(q, h):
            if h == 0:
                unit["w", q] = stage.tile([P, 2, PACK, HALF], BF16, name="unit", bufs=2, align_bytes=64)
            normalise(unit["w", q][:, h, :, :], w_raw[q, h], w_inv, q * PACK)

        def w_interleave(q, h, engine):
            interleave(("w", q), unit["w", q][:, h, :, :], halves[h], engine)

        def w_quantise(q, h):
            quantise(("w", q), halves[h], w_codes[:, q, :], w_scales[:, q, :], E4M3)

        w_normalise(0, 0)
        w_interleave(0, 0, "scalar")
        e_inv = inverse(e_norm[:].rearrange("p g j -> p (g j)"), N // P, "e_inv")
        w_normalise(1, 0)
        consts["emb"] = row_constants(e_inv, N // P, "emb")
        w_normalise(0, 1)
        w_interleave(0, 1, "scalar")
        w_interleave(1, 0, "vector")
        transpose_pair(0)
        copy_pair(0, "head", 0)
        w_quantise(0, 0)
        w_quantise(1, 0)
        w_normalise(1, 1)
        w_quantise(0, 1)
        w_interleave(1, 1, "vector")
        quantise_flipped("head", 0, 2)
        w_quantise(1, 1)

        whole = slice(0, D)

        def g_quantise(g):
            quantise(("g", g), whole, g_codes[:, g, :], g_scales[:, g, :], E5M2)

        def e_quantise(g):
            quantise(("e", g), whole, e_codes[:, g, :], e_scales[:, g, :], E4M3)

        early = sum(WINDOW_TILES)
        late = [("emb", early), ("emb", early + 1), ("w", 0), ("w", 1)]
        rest = list(range(early + 2, N // P))
        for m in range(2, A // P):
            late.append(("w", m))
            behind = A // P - 1 - m
            if behind < len(rest):
                late.append(("emb", rest[len(rest) - 1 - behind]))

        waiting = []
        done = 0
        for g in range(TOKEN_PASSES):
            last = g + 1 == TOKEN_PASSES
            tiles = [("emb", done + t) for t in range(WINDOW_TILES[g])]
            done = done + len(tiles)
            if g > 0:
                quantise_flipped(g - 1, PACK * g - 2, PACK)
                g_quantise(g - 1)
                e_quantise(g - 1)
            if g == 2:
                row_inv = inverse(row_norm[:], A // P, "row_inv")
            if g == 3:
                consts["w"] = row_constants(row_inv, A // P, "w")
            unit["e", g] = stage.tile([P, PACK, D], BF16, name="unit", bufs=2, align_bytes=64)
            normalise(unit["e", g], e_raw[g], e_inv, g * PACK)

            split = GPSIMD_COLS[g]
            interleave(("e", g), unit["e", g][:, :, 0:split], slice(0, split), "gpsimd")
            for tile in waiting:
                gain_gpsimd(tile)
                store(tile)
            for h in range(2):
                interleave(("g", g), g_raw[g][:, :, halves[h]], halves[h], "scalar")
            if g == 1:
                for s in range(A // P // 2):
                    load_w_rows(s)

            multiply(tiles[0])
            multiply(tiles[1])
            transpose_pair(2 * g + 1)
            if last:
                multiply(("w", 0), upto=TOKEN_PASSES - 1)
                copy_pair(2 * g + 1, g, 0)
                multiply(("w", 1), upto=TOKEN_PASSES - 1)
            else:
                transpose_pair(2 * g + 2)
                copy_pair(2 * g + 1, g, 0)
                copy_pair(2 * g + 2, g, 2)
            if g == 0:
                load_g(TOKEN_PASSES - 1)
            if split < D:
                interleave(("e", g), unit["e", g][:, :, split:D], slice(split, D), "scalar")

            row_sums(tiles[0])
            for t in range(1, len(tiles)):
                row_sum(tiles[t], 0)
                early_coefficient(tiles[t - 1])
                row_sum(tiles[t], 1)
                early_finish(tiles[t - 1], 0)
                if t + 1 == len(tiles):
                    early_coefficient(tiles[t])
                early_finish(tiles[t - 1], 1)
            if last:
                multiply(late[0])
            early_finish(tiles[-1], 0)
            early_finish(tiles[-1], 1)
            waiting = tiles

        def late_start(tile):
            late_coefficient(tile)
            scale_scalar(tile)
            term_scalar(tile, whole)
            finish_gpsimd(tile)

        multiply(late[1])
        quantise_flipped(TOKEN_PASSES - 1, N // P - 2, 2)
        g_quantise(TOKEN_PASSES - 1)
        row_sums(late[0])
        e_quantise(TOKEN_PASSES - 1)
        for tile in waiting:
            gain_scalar(tile)
            store(tile)
        late_start(late[0])

        final = len(late) - 1
        for step in range(1, final):
            multiply(late[step + 1])
            row_sums(late[step])
            late_start(late[step])
            if step >= 2:
                finish_vector(late[step - 2], 0)
                store(late[step - 2], halves[0])
            store(late[step - 1], halves[1])
        tile = late[final]
        row_sums(tile)
        late_coefficient(tile)
        term_scalar(tile, halves[0])
        term_scalar(tile, halves[1])
        finish_vector(late[final - 2], 0)
        store(late[final - 2], halves[0])
        finish_vector(late[final - 1], 0)
        for h in range(2):
            store(late[final - 1], halves[h])
        for h in range(2):
            finish_vector(tile, h)
            store(tile, halves[h])
